import numpy as np
import ml_dtypes


def mxq(x, axis, fmt="e4m3"):
    dtype, down = {"e4m3": (ml_dtypes.float8_e4m3fn, 7), "e5m2": (ml_dtypes.float8_e5m2, 14)}[fmt]
    v = np.moveaxis(np.asarray(x, np.float32).astype(ml_dtypes.bfloat16).astype(np.float64), axis, -1)
    blocks = v.reshape(v.shape[:-1] + (-1, 32))
    amax = np.abs(blocks).max(-1, keepdims=True)
    byte = np.maximum(np.where(amax > 0, np.frexp(amax)[1] - 1 + 127, 0) - down, 1)
    scale = np.exp2(byte - 127.0)
    codes = (blocks / scale).astype(np.float32).astype(dtype).astype(np.float64)
    return np.moveaxis((codes * scale).reshape(v.shape), -1, axis)


WIDE = False


def mx_kscale(k):
    if not WIDE:
        return np.ones(k)
    levels = np.array([10, -10, 5, -5, 0])
    a = np.random.permutation(np.resize(levels, k // 512 * 4)).reshape(k // 512, 4)
    idx = np.arange(k)
    return np.exp2(a[idx // 512, idx % 128 // 32])


BF16 = ml_dtypes.bfloat16


def bf(x):
    return np.asarray(x, np.float32).astype(BF16)


def f64(x):
    return np.asarray(x).astype(np.float64)


B, S, FIN, D, AF, F, H = 4, 1024, 128, 1024, 256, 4096, 16
MAX_TIMESCALE = 10000.0
MIN_TIMESCALE = 1.0
EPS = 1e-3


def timing_signal(length, channels):
    num_ts = channels // 2
    log_inc = np.log(MAX_TIMESCALE / MIN_TIMESCALE) / max(num_ts - 1, 1)
    inv_ts = MIN_TIMESCALE * np.exp(np.arange(num_ts) * -log_inc)
    scaled = np.arange(length)[:, None] * inv_ts[None, :]
    return np.concatenate([np.sin(scaled), np.cos(scaled)], axis=1)[None, :, :]


def layer_norm(v, gamma, beta):
    mu = v.mean(-1, keepdims=True)
    var = v.var(-1, keepdims=True)
    return (v - mu) / np.sqrt(var + EPS) * gamma + beta


def setup_inputs():
    r = np.random.standard_normal
    s = mx_kscale(D)
    return {"x": bf(r((B, S, FIN))),
            "W_emb": bf(r((FIN, D)) / np.sqrt(FIN)), "b_emb": bf(0.1 * r(D)),
            "g0": bf((1.0 + 0.1 * r(D)) * s), "beta0": bf(0.1 * r(D) * s),
            "Wq": bf(r((D, AF)) / np.sqrt(D) / s[:, None]), "bq": bf(0.1 * r(AF)),
            "Wk": bf(r((D, AF)) / np.sqrt(D) / s[:, None]), "bk": bf(0.1 * r(AF)),
            "Wv": bf(r((D, AF)) / np.sqrt(D) / s[:, None]), "bv": bf(0.1 * r(AF))}


def reference(x, W_emb, b_emb, g0, beta0, Wq, bq, Wk, bk, Wv, bv):
    h = np.maximum(f64(x) @ f64(W_emb) + f64(b_emb), 0.0)
    h = h + timing_signal(S, D)
    h = layer_norm(h, f64(g0), f64(beta0))
    hq = mxq(h, 2, "e4m3")
    q = (hq @ mxq(f64(Wq), 0, "e4m3")) + f64(bq)
    k = (hq @ mxq(f64(Wk), 0, "e4m3")) + f64(bk)
    v = (hq @ mxq(f64(Wv), 0, "e4m3")) + f64(bv)
    return q, k, v

@@ -1,0 +1,391 @@
+import math
+from contextlib import ExitStack
+
+import concourse.mybir as mybir
+from concourse.masks import make_identity
+
+F32 = mybir.dt.float32
+BF16 = mybir.dt.bfloat16
+I32 = mybir.dt.int32
+U32 = mybir.dt.uint32
+U8 = mybir.dt.uint8
+FP8X4 = mybir.dt.float8_e4m3fn_x4
+ALU = mybir.AluOpType
+FUNC = mybir.ActivationFunctionType
+
+P = 128
+BATCH = 4
+SEQ = 1024
+FIN = 128
+D = 1024
+N_OUT = 256
+N_ALL = 3 * N_OUT
+EPS = 1e-3
+BANK = 512
+HALVES = D // BANK
+PACK = 4
+K_PASS = P * PACK
+PASSES = D // K_PASS
+CHUNKS = D // P
+N_POS = SEQ // P
+GROUP = BATCH * P
+
+FLOPS = 2 * BATCH * SEQ * (FIN * D + D * N_ALL)
+
+N_FREQ = D // 2
+LOG_STEP = math.log(10000.0) / (N_FREQ - 1)
+FINE = 32
+COARSE = N_FREQ // FINE
+HEAD_BITS = 12
+ROUND_TO_INT = 12582912.0
+
+
+def head_of(value):
+    exponent = math.floor(math.log(value) / math.log(2.0))
+    step = 2.0 ** (exponent - HEAD_BITS + 1)
+    return round(value / step) * step
+
+
+def fill_table(nc, heads, tails, values):
+    for i, value in enumerate(values):
+        nc.vector.memset(heads[:, i : i + 1], head_of(value))
+        nc.vector.memset(tails[:, i : i + 1], value - head_of(value))
+
+
+def tile_ffnn_encoder_pa_t_kernel(
+    tc, x, W_emb, b_emb, g0, beta0, Wq, bq, Wk, bk, Wv, bv, out_0, out_1, out_2
+):
+    nc = tc.nc
+    with ExitStack() as ctx:
+        ctx.enter_context(tc.manual_schedule())
+        keep = ctx.enter_context(tc.tile_pool(name="keep", bufs=1))
+        setup = ctx.enter_context(tc.tile_pool(name="setup", bufs=2))
+        angle = ctx.enter_context(tc.tile_pool(name="angle", bufs=2))
+        work = ctx.enter_context(tc.tile_pool(name="work", bufs=2))
+        psum_z = ctx.enter_context(tc.psum_pool(name="psum_z", bufs=2))
+        psum_t = ctx.enter_context(tc.psum_pool(name="psum_t", bufs=4))
+        psum_o = ctx.enter_context(tc.psum_pool(name="psum_o", bufs=1))
+
+        x_by_pos = x.rearrange("b (a p) f -> a p b f", p=P)
+        x_sb = keep.tile([P, N_POS, BATCH, FIN], BF16)
+        nc.sync.dma_start(out=x_sb[:, 0], in_=x_by_pos[0])
+        w_emb = keep.tile([P, D], BF16)
+        nc.sync.dma_start(out=w_emb[:], in_=W_emb)
+        rows = keep.tile([P, P], BF16)
+        nc.vector.memset(rows[:], 0.0)
+        for v, vector in enumerate((b_emb, g0, beta0)):
+            nc.sync.dma_start(
+                out=rows[v * CHUNKS : (v + 1) * CHUNKS, :],
+                in_=vector.rearrange("(c p) -> c p", p=P),
+            )
+        nc.sync.dma_start(out=x_sb[:, 1], in_=x_by_pos[1])
+        w_raw = []
+        for w, weight in enumerate((Wq, Wk, Wv)):
+            raw = setup.tile([P, PASSES, PACK, N_OUT], BF16, name="w_raw%d" % w, tag="w_raw", bufs=3)
+            nc.sync.dma_start(
+                out=raw[:].rearrange("p g t n -> p (g t) n"),
+                in_=weight.rearrange("(c p) n -> p c n", p=P),
+            )
+            w_raw.append(raw)
+        for a in range(2, N_POS):
+            nc.sync.dma_start(out=x_sb[:, a], in_=x_by_pos[a])
+        bias_qkv = keep.tile([P, N_ALL], BF16)
+        for w, vector in enumerate((bq, bk, bv)):
+            nc.sync.dma_start(
+                out=bias_qkv[:, w * N_OUT : (w + 1) * N_OUT], in_=vector.partition_broadcast(P)
+            )
+
+        ident_f = keep.tile([P, P], F32)
+        make_identity(nc, ident_f[:])
+        ident_b = keep.tile([P, P], BF16)
+        make_identity(nc, ident_b[:])
+        pos_i = keep.tile([P, N_POS], I32)
+        nc.gpsimd.iota(out=pos_i[:], pattern=[[P, N_POS]], base=0, channel_multiplier=1)
+        minus_eighth = keep.tile([P, 1], F32)
+        nc.vector.memset(minus_eighth[:], -0.125)
+        plus_eighth = keep.tile([P, 1], F32)
+        nc.vector.memset(plus_eighth[:], 0.125)
+        minus_half = keep.tile([P, BATCH], F32)
+        nc.vector.memset(minus_half[:], -0.5)
+
+        coarse_hd = keep.tile([P, COARSE], F32)
+        coarse_tl = keep.tile([P, COARSE], F32)
+        fill_table(
+            nc, coarse_hd, coarse_tl,
+            [math.exp(-FINE * i * LOG_STEP) / (2.0 * math.pi) for i in range(COARSE)],
+        )
+        fine_hd = keep.tile([P, FINE], F32)
+        fine_tl = keep.tile([P, FINE], F32)
+        fill_table(nc, fine_hd, fine_tl, [math.exp(-i * LOG_STEP) for i in range(FINE)])
+        fine_all = keep.tile([P, FINE], F32)
+        nc.vector.tensor_tensor(out=fine_all[:], in0=fine_hd[:], in1=fine_tl[:], op=ALU.add)
+
+        pos = keep.tile([P, N_POS], F32)
+        nc.vector.tensor_copy(out=pos[:], in_=pos_i[:])
+
+        def over_fine(table):
+            return table[:].unsqueeze(2).to_broadcast([P, COARSE, FINE])
+
+        def over_coarse(table):
+            return table[:].unsqueeze(1).to_broadcast([P, COARSE, FINE])
+
+        def as_grid(tile):
+            return tile[:].rearrange("p (a b) -> p a b", b=FINE)
+
+        product = setup.tile([P, N_FREQ], F32, bufs=1)
+        cross = setup.tile([P, N_FREQ], F32, bufs=1)
+        cross2 = setup.tile([P, N_FREQ], F32, bufs=1)
+        f_head = keep.tile([P, N_FREQ], F32)
+        f_tail = keep.tile([P, N_FREQ], F32)
+        nc.vector.tensor_tensor(
+            out=as_grid(product), in0=over_fine(coarse_hd), in1=over_coarse(fine_hd), op=ALU.mult
+        )
+        nc.vector.tensor_tensor(
+            out=as_grid(cross), in0=over_fine(coarse_hd), in1=over_coarse(fine_tl), op=ALU.mult
+        )
+        nc.vector.tensor_tensor(
+            out=as_grid(cross2), in0=over_fine(coarse_tl), in1=over_coarse(fine_all), op=ALU.mult
+        )
+        nc.vector.tensor_single_scalar(
+            out=f_head[:].bitcast(I32), in_=product[:].bitcast(I32), scalar=-2048, op=ALU.bitwise_and
+        )
+        nc.vector.tensor_tensor(out=cross[:], in0=cross[:], in1=cross2[:], op=ALU.add)
+        nc.vector.tensor_tensor(out=product[:], in0=product[:], in1=f_head[:], op=ALU.subtract)
+        nc.vector.tensor_tensor(out=f_tail[:], in0=product[:], in1=cross[:], op=ALU.add)
+
+        rows_t = psum_t.tile([P, P], BF16, tag="tp")
+        nc.tensor.transpose(out=rows_t[:], in_=rows[:], identity=ident_b[:])
+        cols = keep.tile([P, 3 * CHUNKS], F32)
+        nc.vector.tensor_copy(out=cols[:], in_=rows_t[:, 0 : 3 * CHUNKS])
+        b_wide = keep.tile([P, CHUNKS, P], F32)
+        nc.vector.tensor_copy(
+            out=b_wide[:], in_=cols[:, 0:CHUNKS].unsqueeze(2).to_broadcast([P, CHUNKS, P])
+        )
+
+        w_codes = keep.tile([P, PASSES, N_ALL], U32, align_bytes=64)
+        w_scales = keep.tile([P, PASSES, N_ALL], U8, align_bytes=64)
+        for w in range(3):
+            w_grouped = setup.tile([P, PASSES, N_OUT, PACK], BF16, bufs=3, align_bytes=64)
+            nc.scalar.copy(out=w_grouped[:], in_=w_raw[w][:].rearrange("p g t n -> p g n t"))
+            for g in range(PASSES):
+                cols_w = slice(w * N_OUT, (w + 1) * N_OUT)
+                nc.vector.quantize_mx(
+                    out=w_codes[:, g, cols_w].bitcast(FP8X4),
+                    scales=w_scales[:, g, cols_w],
+                    in_=w_grouped[:, g].rearrange("p n t -> p (n t)"),
+                )
+
+        timing = keep.tile([P, N_POS, D], F32)
+
+        def timing_fraction(a):
+            here = pos[:, a : a + 1]
+            turns = angle.tile([P, N_FREQ], F32)
+            nc.gpsimd.tensor_scalar(
+                out=turns[:], in0=f_head[:], scalar1=here, scalar2=-0.125, op0=ALU.mult, op1=ALU.add
+            )
+            whole = angle.tile([P, N_FREQ], F32)
+            nc.gpsimd.tensor_scalar(
+                out=whole[:], in0=turns[:], scalar1=1.0, scalar2=ROUND_TO_INT, op0=ALU.mult, op1=ALU.add
+            )
+            nc.gpsimd.tensor_scalar(
+                out=whole[:], in0=whole[:], scalar1=-ROUND_TO_INT, scalar2=-1.0, op0=ALU.add, op1=ALU.mult
+            )
+            nc.gpsimd.tensor_tensor(out=whole[:], in0=turns[:], in1=whole[:], op=ALU.add)
+            frac = angle.tile([P, N_FREQ], F32)
+            nc.gpsimd.tensor_scalar(
+                out=frac[:], in0=f_tail[:], scalar1=here, scalar2=0.0, op0=ALU.mult, op1=ALU.add
+            )
+            nc.gpsimd.tensor_tensor(out=frac[:], in0=whole[:], in1=frac[:], op=ALU.add)
+            return frac
+
+        def timing_fold(frac):
+            fold = angle.tile([P, D], F32)
+            nc.scalar.activation(
+                out=fold[:, 0:N_FREQ], in_=frac[:], func=FUNC.Abs, bias=minus_eighth[:], scale=1.0
+            )
+            nc.scalar.activation(
+                out=fold[:, N_FREQ:D], in_=frac[:], func=FUNC.Abs, bias=plus_eighth[:], scale=1.0
+            )
+            nc.gpsimd.tensor_scalar(
+                out=fold[:], in0=fold[:], scalar1=-1.0, scalar2=0.25, op0=ALU.mult, op1=ALU.add
+            )
+            return fold
+
+        def timing_sine(a, fold):
+            nc.scalar.activation(out=timing[:, a, :], in_=fold[:], func=FUNC.Sin, scale=2.0 * math.pi)
+
+        def transpose_x(a):
+            x_t_ps = psum_t.tile([P, GROUP], BF16, tag="tp")
+            for b in range(BATCH):
+                nc.tensor.transpose(
+                    out=x_t_ps[:, b * P : (b + 1) * P], in_=x_sb[:, a, b, :], identity=ident_b[:]
+                )
+            x_t = work.tile([P, GROUP], BF16, bufs=2)
+            nc.scalar.copy(out=x_t[:], in_=x_t_ps[:])
+            return x_t
+
+        def embed(a, b, x_t, sum_e, sum_sq):
+            e = work.tile([P, D], F32, bufs=8)
+            for half in range(HALVES):
+                z = psum_z.tile([P, BANK], F32)
+                for j in range(BANK // P):
+                    nc.tensor.matmul(
+                        out=z[:, j * P : (j + 1) * P],
+                        lhsT=b_wide[:, half * (BANK // P) + j, :],
+                        rhs=ident_f[:],
+                        is_transpose=True,
+                        start=(j == 0),
+                        stop=False,
+                    )
+                nc.tensor.matmul(
+                    out=z[:],
+                    lhsT=x_t[:, b * P : (b + 1) * P],
+                    rhs=w_emb[:, half * BANK : (half + 1) * BANK],
+                    start=False,
+                    stop=True,
+                )
+                nc.vector.scalar_tensor_tensor(
+                    out=e[:, half * BANK : (half + 1) * BANK],
+                    in0=z[:],
+                    scalar=0.0,
+                    in1=timing[:, a, half * BANK : (half + 1) * BANK],
+                    op0=ALU.max,
+                    op1=ALU.add,
+                    accum_out=sum_e[:, b, half : half + 1],
+                )
+            squares = work.tile([P, D], BF16, bufs=2)
+            nc.scalar.activation(
+                out=squares[:], in_=e[:], func=FUNC.Square, accum_out=sum_sq[:, b : b + 1]
+            )
+            return e
+
+        def inverse_deviation(sum_e, sum_sq):
+            total = work.tile([P, BATCH], F32, bufs=3)
+            nc.vector.tensor_tensor(out=total[:], in0=sum_e[:, :, 0], in1=sum_e[:, :, 1], op=ALU.add)
+            minus_mean_sq = work.tile([P, BATCH], F32, bufs=3)
+            nc.vector.scalar_tensor_tensor(
+                out=minus_mean_sq[:], in0=total[:], scalar=-1.0 / (D * D), in1=total[:],
+                op0=ALU.mult, op1=ALU.mult,
+            )
+            var_eps = work.tile([P, BATCH], F32, bufs=3)
+            nc.vector.tensor_scalar(
+                out=var_eps[:], in0=sum_sq[:], scalar1=1.0 / D, scalar2=EPS, op0=ALU.mult, op1=ALU.add
+            )
+            nc.vector.tensor_tensor(out=var_eps[:], in0=var_eps[:], in1=minus_mean_sq[:], op=ALU.add)
+            rstd = work.tile([P, BATCH], F32, bufs=3)
+            nc.gpsimd.tensor_tensor(out=rstd[:], in0=var_eps[:], in1=minus_half[:], op=ALU.pow)
+            return total, rstd
+
+        def normalise(e_tiles, total, rstd):
+            shift = work.tile([P, BATCH], F32, bufs=3)
+            nc.vector.scalar_tensor_tensor(
+                out=shift[:], in0=total[:], scalar=-1.0 / D, in1=rstd[:], op0=ALU.mult, op1=ALU.mult
+            )
+            normed_tiles = []
+            for b in range(BATCH):
+                normed = work.tile([P, D], F32, name="normed%d" % b, tag="normed", bufs=6)
+                nc.gpsimd.tensor_scalar(
+                    out=normed[:], in0=e_tiles[b][:], scalar1=rstd[:, b : b + 1],
+                    scalar2=shift[:, b : b + 1], op0=ALU.mult, op1=ALU.add,
+                )
+                normed_tiles.append(normed)
+            return normed_tiles
+
+        def scale_and_shift(normed_tiles, g):
+            planes = work.tile([P, PACK, GROUP], BF16, bufs=3)
+            for t in range(PACK):
+                c = g * PACK + t
+                normed_t = psum_t.tile([P, GROUP], F32, tag="tp")
+                for b in range(BATCH):
+                    nc.tensor.transpose(
+                        out=normed_t[:, b * P : (b + 1) * P],
+                        in_=normed_tiles[b][:, c * P : (c + 1) * P],
+                        identity=ident_f[:],
+                    )
+                nc.scalar.activation(
+                    out=planes[:, t, :], in_=normed_t[:], func=FUNC.Identity,
+                    scale=cols[:, CHUNKS + c : CHUNKS + c + 1],
+                    bias=cols[:, 2 * CHUNKS + c : 2 * CHUNKS + c + 1],
+                )
+            return planes
+
+        def quantise(planes):
+            grouped = work.tile([P, GROUP, PACK], BF16, bufs=2, align_bytes=64)
+            nc.vector.tensor_copy(out=grouped[:], in_=planes[:].rearrange("p t r -> p r t"))
+            codes = work.tile([P, GROUP], U32, bufs=4, align_bytes=64)
+            scales = work.tile([P, GROUP], U8, bufs=4, align_bytes=64)
+            nc.vector.quantize_mx(
+                out=codes[:].bitcast(FP8X4),
+                scales=scales[:],
+                in_=grouped[:].rearrange("p r t -> p (r t)"),
+            )
+            return codes, scales
+
+        def project(b, h_mx, result):
+            tokens = slice(b * P, (b + 1) * P)
+            for name, first, width in (("acc_qk", 0, BANK), ("acc_v", BANK, N_ALL - BANK)):
+                acc = psum_o.tile([P, width], F32, name=name, tag=name)
+                for g in range(PASSES):
+                    codes, scales = h_mx[g]
+                    nc.tensor.matmul_mx(
+                        out=acc[:],
+                        lhsT=codes[:, tokens].bitcast(FP8X4),
+                        lhsT_scale=scales[:, tokens],
+                        rhs=w_codes[:, g, first : first + width].bitcast(FP8X4),
+                        rhs_scale=w_scales[:, g, first : first + width],
+                        start=(g == 0),
+                        stop=(g == PASSES - 1),
+                    )
+                nc.vector.tensor_tensor(
+                    out=result[:, b, first : first + width], in0=acc[:],
+                    in1=bias_qkv[:, first : first + width], op=ALU.add,
+                )
+
+        x_t_next = transpose_x(0)
+        timing_sine(0, timing_fold(timing_fraction(0)))
+        frac_next = timing_fraction(1)
+        normed_tiles = None
+        for a in range(-1, N_POS):
+            embedding = a + 1 < N_POS
+            finishing = a >= 0
+            x_t = x_t_next
+            h_mx = []
+            e_tiles = []
+            if embedding:
+                sum_e = work.tile([P, BATCH, HALVES], F32, bufs=3)
+                sum_sq = work.tile([P, BATCH], F32, bufs=3)
+                e_tiles.append(embed(a + 1, 0, x_t, sum_e, sum_sq))
+                e_tiles.append(embed(a + 1, 1, x_t, sum_e, sum_sq))
+            if finishing:
+                planes = scale_and_shift(normed_tiles, 0)
+            if embedding:
+                e_tiles.append(embed(a + 1, 2, x_t, sum_e, sum_sq))
+            if finishing:
+                h_mx.append(quantise(planes))
+                planes = scale_and_shift(normed_tiles, 1)
+            if a + 2 < N_POS:
+                fold = timing_fold(frac_next)
+            if embedding:
+                e_tiles.append(embed(a + 1, 3, x_t, sum_e, sum_sq))
+            if finishing:
+                h_mx.append(quantise(planes))
+            if embedding:
+                total, rstd = inverse_deviation(sum_e, sum_sq)
+            if a + 2 < N_POS:
+                timing_sine(a + 2, fold)
+                x_t_next = transpose_x(a + 2)
+            if finishing:
+                result = work.tile([P, BATCH, N_ALL], F32, bufs=2)
+                project(0, h_mx, result)
+            if embedding:
+                normed_tiles = normalise(e_tiles, total, rstd)
+            if a + 3 < N_POS:
+                frac_next = timing_fraction(a + 3)
+            if finishing:
+                for b in range(1, BATCH):
+                    project(b, h_mx, result)
+                for w, out in enumerate((out_0, out_1, out_2)):
+                    nc.sync.dma_start(
+                        out=out.rearrange("b (a p) n -> a p b n", p=P)[a],
+                        in_=result[:, :, w * N_OUT : (w + 1) * N_OUT],
+                    )

@@ -46,10 +46,10 @@ def head_of(value):
     return round(value / step) * step
 
 
-def fill_table(nc, heads, tails, values):
+def fill_table(nc, heads, tails, one, values):
     for i, value in enumerate(values):
         nc.vector.memset(heads[:, i : i + 1], head_of(value))
-        nc.vector.memset(tails[:, i : i + 1], value - head_of(value))
+        nc.scalar.mul(out=tails[:, i : i + 1], in_=one[:], mul=value - head_of(value))
 
 
 def tile_ffnn_encoder_pa_t_kernel(
@@ -59,8 +59,6 @@ def tile_ffnn_encoder_pa_t_kernel(
     with ExitStack() as ctx:
         ctx.enter_context(tc.manual_schedule())
         keep = ctx.enter_context(tc.tile_pool(name="keep", bufs=1))
-        setup = ctx.enter_context(tc.tile_pool(name="setup", bufs=2))
-        angle = ctx.enter_context(tc.tile_pool(name="angle", bufs=2))
         work = ctx.enter_context(tc.tile_pool(name="work", bufs=2))
         psum_z = ctx.enter_context(tc.psum_pool(name="psum_z", bufs=2))
         psum_t = ctx.enter_context(tc.psum_pool(name="psum_t", bufs=4))
@@ -78,50 +76,48 @@ def tile_ffnn_encoder_pa_t_kernel(
                 out=rows[v * CHUNKS : (v + 1) * CHUNKS, :],
                 in_=vector.rearrange("(c p) -> c p", p=P),
             )
-        nc.sync.dma_start(out=x_sb[:, 1], in_=x_by_pos[1])
+        for a in range(1, N_POS):
+            nc.sync.dma_start(out=x_sb[:, a], in_=x_by_pos[a])
         w_raw = []
         for w, weight in enumerate((Wq, Wk, Wv)):
-            raw = setup.tile([P, PASSES, PACK, N_OUT], BF16, name="w_raw%d" % w, tag="w_raw", bufs=3)
+            raw = keep.tile([P, PASSES, PACK, N_OUT], BF16, name="w_raw%d" % w)
             nc.sync.dma_start(
                 out=raw[:].rearrange("p g t n -> p (g t) n"),
                 in_=weight.rearrange("(c p) n -> p c n", p=P),
             )
             w_raw.append(raw)
-        for a in range(2, N_POS):
-            nc.sync.dma_start(out=x_sb[:, a], in_=x_by_pos[a])
         bias_qkv = keep.tile([P, N_ALL], BF16)
         for w, vector in enumerate((bq, bk, bv)):
             nc.sync.dma_start(
                 out=bias_qkv[:, w * N_OUT : (w + 1) * N_OUT], in_=vector.partition_broadcast(P)
             )
 
-        ident_f = keep.tile([P, P], F32)
-        make_identity(nc, ident_f[:])
         ident_b = keep.tile([P, P], BF16)
         make_identity(nc, ident_b[:])
+        ident_f = keep.tile([P, P], F32)
+        make_identity(nc, ident_f[:])
         pos_i = keep.tile([P, N_POS], I32)
         nc.gpsimd.iota(out=pos_i[:], pattern=[[P, N_POS]], base=0, channel_multiplier=1)
+        one = keep.tile([P, 1], F32)
+        nc.vector.memset(one[:], 1.0)
         minus_eighth = keep.tile([P, 1], F32)
         nc.vector.memset(minus_eighth[:], -0.125)
         plus_eighth = keep.tile([P, 1], F32)
         nc.vector.memset(plus_eighth[:], 0.125)
         minus_half = keep.tile([P, BATCH], F32)
         nc.vector.memset(minus_half[:], -0.5)
+        quarter_turn = keep.tile([P, 1], F32)
+        nc.scalar.mul(out=quarter_turn[:], in_=one[:], mul=0.5 * math.pi)
 
         coarse_hd = keep.tile([P, COARSE], F32)
         coarse_tl = keep.tile([P, COARSE], F32)
         fill_table(
-            nc, coarse_hd, coarse_tl,
+            nc, coarse_hd, coarse_tl, one,
             [math.exp(-FINE * i * LOG_STEP) / (2.0 * math.pi) for i in range(COARSE)],
         )
         fine_hd = keep.tile([P, FINE], F32)
         fine_tl = keep.tile([P, FINE], F32)
-        fill_table(nc, fine_hd, fine_tl, [math.exp(-i * LOG_STEP) for i in range(FINE)])
-        fine_all = keep.tile([P, FINE], F32)
-        nc.vector.tensor_tensor(out=fine_all[:], in0=fine_hd[:], in1=fine_tl[:], op=ALU.add)
-
-        pos = keep.tile([P, N_POS], F32)
-        nc.vector.tensor_copy(out=pos[:], in_=pos_i[:])
+        fill_table(nc, fine_hd, fine_tl, one, [math.exp(-i * LOG_STEP) for i in range(FINE)])
 
         def over_fine(table):
             return table[:].unsqueeze(2).to_broadcast([P, COARSE, FINE])
@@ -129,25 +125,29 @@ def tile_ffnn_encoder_pa_t_kernel(
         def over_coarse(table):
             return table[:].unsqueeze(1).to_broadcast([P, COARSE, FINE])
 
-        def as_grid(tile):
-            return tile[:].rearrange("p (a b) -> p a b", b=FINE)
+        def as_grid(flat):
+            return flat[:].rearrange("p (a b) -> p a b", b=FINE)
 
-        product = setup.tile([P, N_FREQ], F32, bufs=1)
-        cross = setup.tile([P, N_FREQ], F32, bufs=1)
-        cross2 = setup.tile([P, N_FREQ], F32, bufs=1)
+        product = keep.tile([P, N_FREQ], F32)
+        cross = keep.tile([P, N_FREQ], F32)
+        cross2 = keep.tile([P, N_FREQ], F32)
         f_head = keep.tile([P, N_FREQ], F32)
         f_tail = keep.tile([P, N_FREQ], F32)
         nc.vector.tensor_tensor(
             out=as_grid(product), in0=over_fine(coarse_hd), in1=over_coarse(fine_hd), op=ALU.mult
         )
+        nc.vector.tensor_single_scalar(
+            out=f_head[:].bitcast(I32), in_=product[:].bitcast(I32), scalar=-2048, op=ALU.bitwise_and
+        )
+        pos = keep.tile([P, N_POS], F32)
+        nc.vector.tensor_copy(out=pos[:], in_=pos_i[:])
+        fine_all = keep.tile([P, FINE], F32)
+        nc.vector.tensor_tensor(out=fine_all[:], in0=fine_hd[:], in1=fine_tl[:], op=ALU.add)
         nc.vector.tensor_tensor(
             out=as_grid(cross), in0=over_fine(coarse_hd), in1=over_coarse(fine_tl), op=ALU.mult
         )
         nc.vector.tensor_tensor(
             out=as_grid(cross2), in0=over_fine(coarse_tl), in1=over_coarse(fine_all), op=ALU.mult
-        )
-        nc.vector.tensor_single_scalar(
-            out=f_head[:].bitcast(I32), in_=product[:].bitcast(I32), scalar=-2048, op=ALU.bitwise_and
         )
         nc.vector.tensor_tensor(out=cross[:], in0=cross[:], in1=cross2[:], op=ALU.add)
         nc.vector.tensor_tensor(out=product[:], in0=product[:], in1=f_head[:], op=ALU.subtract)
@@ -164,9 +164,13 @@ def tile_ffnn_encoder_pa_t_kernel(
 
         w_codes = keep.tile([P, PASSES, N_ALL], U32, align_bytes=64)
         w_scales = keep.tile([P, PASSES, N_ALL], U8, align_bytes=64)
-        for w in range(3):
-            w_grouped = setup.tile([P, PASSES, N_OUT, PACK], BF16, bufs=3, align_bytes=64)
+
+        def regroup_weight(w):
+            w_grouped = work.tile([P, PASSES, N_OUT, PACK], BF16, bufs=2, align_bytes=64)
             nc.scalar.copy(out=w_grouped[:], in_=w_raw[w][:].rearrange("p g t n -> p g n t"))
+            return w_grouped
+
+        def quantise_weight(w, w_grouped):
             for g in range(PASSES):
                 cols_w = slice(w * N_OUT, (w + 1) * N_OUT)
                 nc.vector.quantize_mx(
@@ -179,11 +183,11 @@ def tile_ffnn_encoder_pa_t_kernel(
 
         def timing_fraction(a):
             here = pos[:, a : a + 1]
-            turns = angle.tile([P, N_FREQ], F32)
+            turns = work.tile([P, N_FREQ], F32, bufs=1)
             nc.gpsimd.tensor_scalar(
                 out=turns[:], in0=f_head[:], scalar1=here, scalar2=-0.125, op0=ALU.mult, op1=ALU.add
             )
-            whole = angle.tile([P, N_FREQ], F32)
+            whole = work.tile([P, N_FREQ], F32, bufs=1)
             nc.gpsimd.tensor_scalar(
                 out=whole[:], in0=turns[:], scalar1=1.0, scalar2=ROUND_TO_INT, op0=ALU.mult, op1=ALU.add
             )
@@ -191,28 +195,25 @@ def tile_ffnn_encoder_pa_t_kernel(
                 out=whole[:], in0=whole[:], scalar1=-ROUND_TO_INT, scalar2=-1.0, op0=ALU.add, op1=ALU.mult
             )
             nc.gpsimd.tensor_tensor(out=whole[:], in0=turns[:], in1=whole[:], op=ALU.add)
-            frac = angle.tile([P, N_FREQ], F32)
+            frac = work.tile([P, N_FREQ], F32, bufs=2)
             nc.gpsimd.tensor_scalar(
                 out=frac[:], in0=f_tail[:], scalar1=here, scalar2=0.0, op0=ALU.mult, op1=ALU.add
             )
             nc.gpsimd.tensor_tensor(out=frac[:], in0=whole[:], in1=frac[:], op=ALU.add)
             return frac
 
-        def timing_fold(frac):
-            fold = angle.tile([P, D], F32)
+        def timing_sines(a, frac):
+            distance = work.tile([P, D], F32, bufs=1)
             nc.scalar.activation(
-                out=fold[:, 0:N_FREQ], in_=frac[:], func=FUNC.Abs, bias=minus_eighth[:], scale=1.0
+                out=distance[:, 0:N_FREQ], in_=frac[:], func=FUNC.Abs, bias=minus_eighth[:], scale=1.0
             )
             nc.scalar.activation(
-                out=fold[:, N_FREQ:D], in_=frac[:], func=FUNC.Abs, bias=plus_eighth[:], scale=1.0
+                out=distance[:, N_FREQ:D], in_=frac[:], func=FUNC.Abs, bias=plus_eighth[:], scale=1.0
             )
-            nc.gpsimd.tensor_scalar(
-                out=fold[:], in0=fold[:], scalar1=-1.0, scalar2=0.25, op0=ALU.mult, op1=ALU.add
+            nc.scalar.activation(
+                out=timing[:, a, :], in_=distance[:], func=FUNC.Sin,
+                bias=quarter_turn[:], scale=-2.0 * math.pi,
             )
-            return fold
-
-        def timing_sine(a, fold):
-            nc.scalar.activation(out=timing[:, a, :], in_=fold[:], func=FUNC.Sin, scale=2.0 * math.pi)
 
         def transpose_x(a):
             x_t_ps = psum_t.tile([P, GROUP], BF16, tag="tp")
@@ -224,40 +225,39 @@ def tile_ffnn_encoder_pa_t_kernel(
             nc.scalar.copy(out=x_t[:], in_=x_t_ps[:])
             return x_t
 
-        def embed(a, b, x_t, sum_e, sum_sq):
-            e = work.tile([P, D], F32, bufs=8)
-            for half in range(HALVES):
-                z = psum_z.tile([P, BANK], F32)
-                for j in range(BANK // P):
-                    nc.tensor.matmul(
-                        out=z[:, j * P : (j + 1) * P],
-                        lhsT=b_wide[:, half * (BANK // P) + j, :],
-                        rhs=ident_f[:],
-                        is_transpose=True,
-                        start=(j == 0),
-                        stop=False,
-                    )
+        def embed_bank(a, b, half, x_t, e, sum_e):
+            z = psum_z.tile([P, BANK], F32)
+            for j in range(BANK // P):
                 nc.tensor.matmul(
-                    out=z[:],
-                    lhsT=x_t[:, b * P : (b + 1) * P],
-                    rhs=w_emb[:, half * BANK : (half + 1) * BANK],
-                    start=False,
-                    stop=True,
+                    out=z[:, j * P : (j + 1) * P],
+                    lhsT=b_wide[:, half * (BANK // P) + j, :],
+                    rhs=ident_f[:],
+                    is_transpose=True,
+                    start=(j == 0),
+                    stop=False,
                 )
-                nc.vector.scalar_tensor_tensor(
-                    out=e[:, half * BANK : (half + 1) * BANK],
-                    in0=z[:],
-                    scalar=0.0,
-                    in1=timing[:, a, half * BANK : (half + 1) * BANK],
-                    op0=ALU.max,
-                    op1=ALU.add,
-                    accum_out=sum_e[:, b, half : half + 1],
-                )
+            nc.tensor.matmul(
+                out=z[:],
+                lhsT=x_t[:, b * P : (b + 1) * P],
+                rhs=w_emb[:, half * BANK : (half + 1) * BANK],
+                start=False,
+                stop=True,
+            )
+            nc.vector.scalar_tensor_tensor(
+                out=e[:, half * BANK : (half + 1) * BANK],
+                in0=z[:],
+                scalar=0.0,
+                in1=timing[:, a, half * BANK : (half + 1) * BANK],
+                op0=ALU.max,
+                op1=ALU.add,
+                accum_out=sum_e[:, b, half : half + 1],
+            )
+
+        def sum_of_squares(e, b, sum_sq):
             squares = work.tile([P, D], BF16, bufs=2)
             nc.scalar.activation(
                 out=squares[:], in_=e[:], func=FUNC.Square, accum_out=sum_sq[:, b : b + 1]
             )
-            return e
 
         def inverse_deviation(sum_e, sum_sq):
             total = work.tile([P, BATCH], F32, bufs=3)
@@ -276,14 +276,17 @@ def tile_ffnn_encoder_pa_t_kernel(
             nc.gpsimd.tensor_tensor(out=rstd[:], in0=var_eps[:], in1=minus_half[:], op=ALU.pow)
             return total, rstd
 
-        def normalise(e_tiles, total, rstd):
+        def minus_mean_rstd(total, rstd):
             shift = work.tile([P, BATCH], F32, bufs=3)
             nc.vector.scalar_tensor_tensor(
                 out=shift[:], in0=total[:], scalar=-1.0 / D, in1=rstd[:], op0=ALU.mult, op1=ALU.mult
             )
+            return shift
+
+        def normalise(e_tiles, rstd, shift):
             normed_tiles = []
             for b in range(BATCH):
-                normed = work.tile([P, D], F32, name="normed%d" % b, tag="normed", bufs=6)
+                normed = work.tile([P, D], F32, name="normed%d" % b, tag="normed", bufs=8)
                 nc.gpsimd.tensor_scalar(
                     out=normed[:], in0=e_tiles[b][:], scalar1=rstd[:, b : b + 1],
                     scalar2=shift[:, b : b + 1], op0=ALU.mult, op1=ALU.add,
@@ -291,23 +294,19 @@ def tile_ffnn_encoder_pa_t_kernel(
                 normed_tiles.append(normed)
             return normed_tiles
 
-        def scale_and_shift(normed_tiles, g):
-            planes = work.tile([P, PACK, GROUP], BF16, bufs=3)
-            for t in range(PACK):
-                c = g * PACK + t
-                normed_t = psum_t.tile([P, GROUP], F32, tag="tp")
-                for b in range(BATCH):
-                    nc.tensor.transpose(
-                        out=normed_t[:, b * P : (b + 1) * P],
-                        in_=normed_tiles[b][:, c * P : (c + 1) * P],
-                        identity=ident_f[:],
-                    )
-                nc.scalar.activation(
-                    out=planes[:, t, :], in_=normed_t[:], func=FUNC.Identity,
-                    scale=cols[:, CHUNKS + c : CHUNKS + c + 1],
-                    bias=cols[:, 2 * CHUNKS + c : 2 * CHUNKS + c + 1],
+        def scale_and_shift(normed_tiles, c, planes):
+            normed_t = psum_t.tile([P, GROUP], F32, tag="tp")
+            for b in range(BATCH):
+                nc.tensor.transpose(
+                    out=normed_t[:, b * P : (b + 1) * P],
+                    in_=normed_tiles[b][:, c * P : (c + 1) * P],
+                    identity=ident_f[:],
                 )
-            return planes
+            nc.scalar.activation(
+                out=planes[:, c % PACK, :], in_=normed_t[:], func=FUNC.Identity,
+                scale=cols[:, CHUNKS + c : CHUNKS + c + 1],
+                bias=cols[:, 2 * CHUNKS + c : 2 * CHUNKS + c + 1],
+            )
 
         def quantise(planes):
             grouped = work.tile([P, GROUP, PACK], BF16, bufs=2, align_bytes=64)
@@ -342,50 +341,65 @@ def tile_ffnn_encoder_pa_t_kernel(
                 )
 
         x_t_next = transpose_x(0)
-        timing_sine(0, timing_fold(timing_fraction(0)))
+        timing_sines(0, timing_fraction(0))
         frac_next = timing_fraction(1)
-        normed_tiles = None
-        for a in range(-1, N_POS):
-            embedding = a + 1 < N_POS
-            finishing = a >= 0
+        stats = {}
+        e_of = {}
+        normed_of = {}
+        h_mx_of = {}
+        for r in range(N_POS + 3):
+            embedding = r < N_POS
+            normalising = 0 <= r - 1 < N_POS
+            quantising = 0 <= r - 2 < N_POS
+            projecting = 0 <= r - 3 < N_POS
             x_t = x_t_next
-            h_mx = []
-            e_tiles = []
+            if normalising:
+                normed_of[r - 1] = normalise(e_of[r - 1], stats[r - 1][0], stats[r - 1][1])
+            if r + 2 < N_POS:
+                frac_after = timing_fraction(r + 2)
             if embedding:
                 sum_e = work.tile([P, BATCH, HALVES], F32, bufs=3)
                 sum_sq = work.tile([P, BATCH], F32, bufs=3)
-                e_tiles.append(embed(a + 1, 0, x_t, sum_e, sum_sq))
-                e_tiles.append(embed(a + 1, 1, x_t, sum_e, sum_sq))
-            if finishing:
-                planes = scale_and_shift(normed_tiles, 0)
-            if embedding:
-                e_tiles.append(embed(a + 1, 2, x_t, sum_e, sum_sq))
-            if finishing:
-                h_mx.append(quantise(planes))
-                planes = scale_and_shift(normed_tiles, 1)
-            if a + 2 < N_POS:
-                fold = timing_fold(frac_next)
-            if embedding:
-                e_tiles.append(embed(a + 1, 3, x_t, sum_e, sum_sq))
-            if finishing:
-                h_mx.append(quantise(planes))
+                e_of[r] = []
+            if quantising:
+                h_mx_of[r - 2] = []
+            for b in range(BATCH):
+                if embedding:
+                    e = work.tile([P, D], F32, bufs=8)
+                    e_of[r].append(e)
+                for half in range(HALVES):
+                    c = b * HALVES + half
+                    if embedding:
+                        embed_bank(r, b, half, x_t, e, sum_e)
+                    if quantising:
+                        if c % PACK == 0:
+                            planes = work.tile([P, PACK, GROUP], BF16, bufs=2)
+                        scale_and_shift(normed_of[r - 2], c, planes)
+                if embedding:
+                    sum_of_squares(e, b, sum_sq)
+                if quantising and c % PACK == PACK - 1:
+                    h_mx_of[r - 2].append(quantise(planes))
+            if r + 1 < N_POS:
+                timing_sines(r + 1, frac_next)
+                x_t_next = transpose_x(r + 1)
+            if r + 2 < N_POS:
+                frac_next = frac_after
             if embedding:
                 total, rstd = inverse_deviation(sum_e, sum_sq)
-            if a + 2 < N_POS:
-                timing_sine(a + 2, fold)
-                x_t_next = transpose_x(a + 2)
-            if finishing:
+            if 1 <= r < 4:
+                quantise_weight(r - 1, w_grouped)
+            if r < 3:
+                w_grouped = regroup_weight(r)
+            if projecting:
                 result = work.tile([P, BATCH, N_ALL], F32, bufs=2)
-                project(0, h_mx, result)
+                project(0, h_mx_of[r - 3], result)
             if embedding:
-                normed_tiles = normalise(e_tiles, total, rstd)
-            if a + 3 < N_POS:
-                frac_next = timing_fraction(a + 3)
-            if finishing:
+                stats[r] = (rstd, minus_mean_rstd(total, rstd))
+            if projecting:
                 for b in range(1, BATCH):
-                    project(b, h_mx, result)
+                    project(b, h_mx_of[r - 3], result)
                 for w, out in enumerate((out_0, out_1, out_2)):
                     nc.sync.dma_start(
-                        out=out.rearrange("b (a p) n -> a p b n", p=P)[a],
+                        out=out.rearrange("b (a p) n -> a p b n", p=P)[r - 3],
                         in_=result[:, :, w * N_OUT : (w + 1) * N_OUT],
                     )

@@ -340,66 +340,81 @@ def tile_ffnn_encoder_pa_t_kernel(
                     in1=bias_qkv[:, first : first + width], op=ALU.add,
                 )
 
-        x_t_next = transpose_x(0)
+        STATS_AT = BATCH
+        NORM_AT = BATCH + 1
+        CHUNKS_AT = 2 * BATCH
+        PROJECT_AT = 3 * BATCH + 1
+        CHUNKS_A_STEP = CHUNKS // BATCH
+
+        def group_at(step, lag):
+            group, place = divmod(step - lag, BATCH)
+            return (group if 0 <= group < N_POS else None), place
+
+        x_t_of = {0: transpose_x(0)}
         timing_sines(0, timing_fraction(0))
-        frac_next = timing_fraction(1)
-        stats = {}
+        frac_of = {1: timing_fraction(1)}
+        sums_of = {}
         e_of = {}
+        stats_of = {}
         normed_of = {}
         h_mx_of = {}
-        for r in range(N_POS + 3):
-            embedding = r < N_POS
-            normalising = 0 <= r - 1 < N_POS
-            quantising = 0 <= r - 2 < N_POS
-            projecting = 0 <= r - 3 < N_POS
-            x_t = x_t_next
-            if normalising:
-                normed_of[r - 1] = normalise(e_of[r - 1], stats[r - 1][0], stats[r - 1][1])
-            if r + 2 < N_POS:
-                frac_after = timing_fraction(r + 2)
-            if embedding:
-                sum_e = work.tile([P, BATCH, HALVES], F32, bufs=3)
-                sum_sq = work.tile([P, BATCH], F32, bufs=3)
-                e_of[r] = []
-            if quantising:
-                h_mx_of[r - 2] = []
-            for b in range(BATCH):
-                if embedding:
-                    e = work.tile([P, D], F32, bufs=8)
-                    e_of[r].append(e)
+        w_grouped_of = {}
+        waiting = None
+        for step in range(BATCH * N_POS + PROJECT_AT):
+            group, b = group_at(step, 0)
+            if group is not None:
+                if b == 0:
+                    sum_e = work.tile([P, BATCH, HALVES], F32, bufs=3)
+                    sum_sq = work.tile([P, BATCH], F32, bufs=3)
+                    sums_of[group] = (sum_e, sum_sq)
+                    e_of[group] = []
+                e = work.tile([P, D], F32, bufs=8)
+                e_of[group].append(e)
                 for half in range(HALVES):
-                    c = b * HALVES + half
-                    if embedding:
-                        embed_bank(r, b, half, x_t, e, sum_e)
-                    if quantising:
-                        if c % PACK == 0:
-                            planes = work.tile([P, PACK, GROUP], BF16, bufs=2)
-                        scale_and_shift(normed_of[r - 2], c, planes)
-                if embedding:
-                    sum_of_squares(e, b, sum_sq)
-                if quantising and c % PACK == PACK - 1:
-                    h_mx_of[r - 2].append(quantise(planes))
-            if r + 1 < N_POS:
-                timing_sines(r + 1, frac_next)
-                x_t_next = transpose_x(r + 1)
-            if r + 2 < N_POS:
-                frac_next = frac_after
-            if embedding:
-                total, rstd = inverse_deviation(sum_e, sum_sq)
-            if 1 <= r < 4:
-                quantise_weight(r - 1, w_grouped)
-            if r < 3:
-                w_grouped = regroup_weight(r)
-            if projecting:
-                result = work.tile([P, BATCH, N_ALL], F32, bufs=2)
-                project(0, h_mx_of[r - 3], result)
-            if embedding:
-                stats[r] = (rstd, minus_mean_rstd(total, rstd))
-            if projecting:
-                for b in range(1, BATCH):
-                    project(b, h_mx_of[r - 3], result)
-                for w, out in enumerate((out_0, out_1, out_2)):
-                    nc.sync.dma_start(
-                        out=out.rearrange("b (a p) n -> a p b n", p=P)[r - 3],
-                        in_=result[:, :, w * N_OUT : (w + 1) * N_OUT],
-                    )
+                    embed_bank(group, b, half, x_t_of[group], e, sums_of[group][0])
+
+            done, place = group_at(step, STATS_AT)
+            if done is not None and place == 0:
+                stats_of[done] = inverse_deviation(sums_of[done][0], sums_of[done][1])
+            done, place = group_at(step, NORM_AT)
+            if done is not None and place == 0:
+                total, rstd = stats_of[done]
+                normed_of[done] = normalise(e_of[done], rstd, minus_mean_rstd(total, rstd))
+            if group is not None and b == 1 and group + 2 < N_POS:
+                frac_of[group + 2] = timing_fraction(group + 2)
+            if group is not None and b == 1 and 1 <= group <= 3:
+                quantise_weight(group - 1, w_grouped_of[group - 1])
+
+            if waiting is not None:
+                h_mx_of[waiting[0]].append(quantise(waiting[1]))
+                waiting = None
+            turned, j = group_at(step, CHUNKS_AT)
+            if turned is not None:
+                for c in range(j * CHUNKS_A_STEP, (j + 1) * CHUNKS_A_STEP):
+                    if c == 0:
+                        h_mx_of[turned] = []
+                    if c % PACK == 0:
+                        planes = work.tile([P, PACK, GROUP], BF16, bufs=2)
+                    scale_and_shift(normed_of[turned], c, planes)
+                    if c % PACK == PACK - 1:
+                        waiting = (turned, planes)
+
+            if group is not None:
+                sum_of_squares(e, b, sums_of[group][1])
+                if b == 2 and group + 1 < N_POS:
+                    timing_sines(group + 1, frac_of[group + 1])
+                    x_t_of[group + 1] = transpose_x(group + 1)
+                if b == 3 and group < 3:
+                    w_grouped_of[group] = regroup_weight(group)
+
+            ready, tile_b = group_at(step, PROJECT_AT)
+            if ready is not None:
+                if tile_b == 0:
+                    result = work.tile([P, BATCH, N_ALL], F32, bufs=2)
+                project(tile_b, h_mx_of[ready], result)
+                if tile_b == BATCH - 1:
+                    for w, out in enumerate((out_0, out_1, out_2)):
+                        nc.sync.dma_start(
+                            out=out.rearrange("b (a p) n -> a p b n", p=P)[ready],
+                            in_=result[:, :, w * N_OUT : (w + 1) * N_OUT],
+                        )

@@ -181,29 +181,23 @@ def tile_ffnn_encoder_pa_t_kernel(
 
         timing = keep.tile([P, N_POS, D], F32)
 
-        def timing_fraction(a):
+        def make_timing(a):
             here = pos[:, a : a + 1]
-            turns = work.tile([P, N_FREQ], F32, bufs=1)
-            nc.gpsimd.tensor_scalar(
+            turns = work.tile([P, N_FREQ], F32, bufs=2)
+            nc.vector.tensor_scalar(
                 out=turns[:], in0=f_head[:], scalar1=here, scalar2=-0.125, op0=ALU.mult, op1=ALU.add
             )
-            whole = work.tile([P, N_FREQ], F32, bufs=1)
-            nc.gpsimd.tensor_scalar(
-                out=whole[:], in0=turns[:], scalar1=1.0, scalar2=ROUND_TO_INT, op0=ALU.mult, op1=ALU.add
+            whole = work.tile([P, N_FREQ], F32, bufs=2)
+            nc.vector.tensor_scalar(
+                out=whole[:], in0=turns[:], scalar1=ROUND_TO_INT, scalar2=ROUND_TO_INT,
+                op0=ALU.add, op1=ALU.subtract,
             )
-            nc.gpsimd.tensor_scalar(
-                out=whole[:], in0=whole[:], scalar1=-ROUND_TO_INT, scalar2=-1.0, op0=ALU.add, op1=ALU.mult
-            )
-            nc.gpsimd.tensor_tensor(out=whole[:], in0=turns[:], in1=whole[:], op=ALU.add)
+            nc.vector.tensor_tensor(out=whole[:], in0=turns[:], in1=whole[:], op=ALU.subtract)
             frac = work.tile([P, N_FREQ], F32, bufs=2)
-            nc.gpsimd.tensor_scalar(
-                out=frac[:], in0=f_tail[:], scalar1=here, scalar2=0.0, op0=ALU.mult, op1=ALU.add
+            nc.vector.scalar_tensor_tensor(
+                out=frac[:], in0=f_tail[:], scalar=here, in1=whole[:], op0=ALU.mult, op1=ALU.add
             )
-            nc.gpsimd.tensor_tensor(out=frac[:], in0=whole[:], in1=frac[:], op=ALU.add)
-            return frac
-
-        def timing_sines(a, frac):
-            distance = work.tile([P, D], F32, bufs=1)
+            distance = work.tile([P, D], F32, bufs=2)
             nc.scalar.activation(
                 out=distance[:, 0:N_FREQ], in_=frac[:], func=FUNC.Abs, bias=minus_eighth[:], scale=1.0
             )
@@ -259,31 +253,24 @@ def tile_ffnn_encoder_pa_t_kernel(
                 out=squares[:], in_=e[:], func=FUNC.Square, accum_out=sum_sq[:, b : b + 1]
             )
 
-        def inverse_deviation(sum_e, sum_sq):
-            total = work.tile([P, BATCH], F32, bufs=3)
-            nc.vector.tensor_tensor(out=total[:], in0=sum_e[:, :, 0], in1=sum_e[:, :, 1], op=ALU.add)
-            minus_mean_sq = work.tile([P, BATCH], F32, bufs=3)
-            nc.vector.scalar_tensor_tensor(
-                out=minus_mean_sq[:], in0=total[:], scalar=-1.0 / (D * D), in1=total[:],
-                op0=ALU.mult, op1=ALU.mult,
+        def normalise(e_tiles, sum_e, sum_sq):
+            total = work.tile([P, BATCH], F32, bufs=2)
+            nc.gpsimd.tensor_tensor(out=total[:], in0=sum_e[:, :, 0], in1=sum_e[:, :, 1], op=ALU.add)
+            minus_mean = work.tile([P, BATCH], F32, bufs=2)
+            nc.gpsimd.tensor_scalar(
+                out=minus_mean[:], in0=total[:], scalar1=-1.0 / D, scalar2=0.0, op0=ALU.mult, op1=ALU.add
             )
-            var_eps = work.tile([P, BATCH], F32, bufs=3)
-            nc.vector.tensor_scalar(
+            mean_sq = work.tile([P, BATCH], F32, bufs=2)
+            nc.gpsimd.tensor_tensor(out=mean_sq[:], in0=minus_mean[:], in1=minus_mean[:], op=ALU.mult)
+            var_eps = work.tile([P, BATCH], F32, bufs=2)
+            nc.gpsimd.tensor_scalar(
                 out=var_eps[:], in0=sum_sq[:], scalar1=1.0 / D, scalar2=EPS, op0=ALU.mult, op1=ALU.add
             )
-            nc.vector.tensor_tensor(out=var_eps[:], in0=var_eps[:], in1=minus_mean_sq[:], op=ALU.add)
-            rstd = work.tile([P, BATCH], F32, bufs=3)
+            nc.gpsimd.tensor_tensor(out=var_eps[:], in0=var_eps[:], in1=mean_sq[:], op=ALU.subtract)
+            rstd = work.tile([P, BATCH], F32, bufs=2)
             nc.gpsimd.tensor_tensor(out=rstd[:], in0=var_eps[:], in1=minus_half[:], op=ALU.pow)
-            return total, rstd
-
-        def minus_mean_rstd(total, rstd):
-            shift = work.tile([P, BATCH], F32, bufs=3)
-            nc.vector.scalar_tensor_tensor(
-                out=shift[:], in0=total[:], scalar=-1.0 / D, in1=rstd[:], op0=ALU.mult, op1=ALU.mult
-            )
-            return shift
-
-        def normalise(e_tiles, rstd, shift):
+            shift = work.tile([P, BATCH], F32, bufs=2)
+            nc.gpsimd.tensor_tensor(out=shift[:], in0=minus_mean[:], in1=rstd[:], op=ALU.mult)
             normed_tiles = []
             for b in range(BATCH):
                 normed = work.tile([P, D], F32, name="normed%d" % b, tag="normed", bufs=8)
@@ -308,9 +295,12 @@ def tile_ffnn_encoder_pa_t_kernel(
                 bias=cols[:, 2 * CHUNKS + c : 2 * CHUNKS + c + 1],
             )
 
-        def quantise(planes):
+        def regroup(planes):
             grouped = work.tile([P, GROUP, PACK], BF16, bufs=2, align_bytes=64)
             nc.vector.tensor_copy(out=grouped[:], in_=planes[:].rearrange("p t r -> p r t"))
+            return grouped
+
+        def quantise(grouped):
             codes = work.tile([P, GROUP], U32, bufs=4, align_bytes=64)
             scales = work.tile([P, GROUP], U8, bufs=4, align_bytes=64)
             nc.vector.quantize_mx(
@@ -340,8 +330,7 @@ def tile_ffnn_encoder_pa_t_kernel(
                     in1=bias_qkv[:, first : first + width], op=ALU.add,
                 )
 
-        STATS_AT = BATCH
-        NORM_AT = BATCH + 1
+        NORM_AT = BATCH
         CHUNKS_AT = 2 * BATCH
         PROJECT_AT = 3 * BATCH + 1
         CHUNKS_A_STEP = CHUNKS // BATCH
@@ -351,11 +340,9 @@ def tile_ffnn_encoder_pa_t_kernel(
             return (group if 0 <= group < N_POS else None), place
 
         x_t_of = {0: transpose_x(0)}
-        timing_sines(0, timing_fraction(0))
-        frac_of = {1: timing_fraction(1)}
+        make_timing(0)
         sums_of = {}
         e_of = {}
-        stats_of = {}
         normed_of = {}
         h_mx_of = {}
         w_grouped_of = {}
@@ -372,22 +359,18 @@ def tile_ffnn_encoder_pa_t_kernel(
                 e_of[group].append(e)
                 for half in range(HALVES):
                     embed_bank(group, b, half, x_t_of[group], e, sums_of[group][0])
+            if step + 1 < N_POS:
+                make_timing(step + 1)
 
-            done, place = group_at(step, STATS_AT)
-            if done is not None and place == 0:
-                stats_of[done] = inverse_deviation(sums_of[done][0], sums_of[done][1])
             done, place = group_at(step, NORM_AT)
             if done is not None and place == 0:
-                total, rstd = stats_of[done]
-                normed_of[done] = normalise(e_of[done], rstd, minus_mean_rstd(total, rstd))
-            if group is not None and b == 1 and group + 2 < N_POS:
-                frac_of[group + 2] = timing_fraction(group + 2)
+                normed_of[done] = normalise(e_of[done], sums_of[done][0], sums_of[done][1])
             if group is not None and b == 1 and 1 <= group <= 3:
                 quantise_weight(group - 1, w_grouped_of[group - 1])
 
+            grouped = None
             if waiting is not None:
-                h_mx_of[waiting[0]].append(quantise(waiting[1]))
-                waiting = None
+                grouped = regroup(waiting[1])
             turned, j = group_at(step, CHUNKS_AT)
             if turned is not None:
                 for c in range(j * CHUNKS_A_STEP, (j + 1) * CHUNKS_A_STEP):
@@ -396,13 +379,10 @@ def tile_ffnn_encoder_pa_t_kernel(
                     if c % PACK == 0:
                         planes = work.tile([P, PACK, GROUP], BF16, bufs=2)
                     scale_and_shift(normed_of[turned], c, planes)
-                    if c % PACK == PACK - 1:
-                        waiting = (turned, planes)
 
             if group is not None:
                 sum_of_squares(e, b, sums_of[group][1])
                 if b == 2 and group + 1 < N_POS:
-                    timing_sines(group + 1, frac_of[group + 1])
                     x_t_of[group + 1] = transpose_x(group + 1)
                 if b == 3 and group < 3:
                     w_grouped_of[group] = regroup_weight(group)
@@ -418,3 +398,8 @@ def tile_ffnn_encoder_pa_t_kernel(
                             out=out.rearrange("b (a p) n -> a p b n", p=P)[ready],
                             in_=result[:, :, w * N_OUT : (w + 1) * N_OUT],
                         )
+            if grouped is not None:
+                h_mx_of[waiting[0]].append(quantise(grouped))
+                waiting = None
+            if turned is not None and (j + 1) * CHUNKS_A_STEP % PACK == 0:
+                waiting = (turned, planes)

@@ -297,7 +297,10 @@ def tile_ffnn_encoder_pa_t_kernel(
 
         def regroup(planes):
             grouped = work.tile([P, GROUP, PACK], BF16, bufs=2, align_bytes=64)
-            nc.vector.tensor_copy(out=grouped[:], in_=planes[:].rearrange("p t r -> p r t"))
+            nc.vector.tensor_copy(
+                out=grouped[:].rearrange("p (c i) t -> p c t i", i=PACK),
+                in_=planes[:].rearrange("p t (c i) -> p c t i", i=PACK),
+            )
             return grouped
 
         def quantise(grouped):
@@ -312,8 +315,9 @@ def tile_ffnn_encoder_pa_t_kernel(
 
         def project(b, h_mx, result):
             tokens = slice(b * P, (b + 1) * P)
-            for name, first, width in (("acc_qk", 0, BANK), ("acc_v", BANK, N_ALL - BANK)):
-                acc = psum_o.tile([P, width], F32, name=name, tag=name)
+
+            def passes(acc, first):
+                width = acc.shape[1]
                 for g in range(PASSES):
                     codes, scales = h_mx[g]
                     nc.tensor.matmul_mx(
@@ -325,10 +329,19 @@ def tile_ffnn_encoder_pa_t_kernel(
                         start=(g == 0),
                         stop=(g == PASSES - 1),
                     )
-                nc.vector.tensor_tensor(
-                    out=result[:, b, first : first + width], in0=acc[:],
-                    in1=bias_qkv[:, first : first + width], op=ALU.add,
-                )
+
+            acc_qk = psum_o.tile([P, BANK], F32)
+            passes(acc_qk, 0)
+            nc.vector.tensor_tensor(
+                out=result[:, b, 0:BANK], in0=acc_qk[:], in1=bias_qkv[:, 0:BANK], op=ALU.add
+            )
+            acc_v = psum_o.tile([P, N_ALL - BANK], F32)
+            passes(acc_v, BANK)
+            v_plain = work.tile([P, N_ALL - BANK], F32, bufs=4)
+            nc.scalar.copy(out=v_plain[:], in_=acc_v[:])
+            nc.gpsimd.tensor_tensor(
+                out=result[:, b, BANK:N_ALL], in0=v_plain[:], in1=bias_qkv[:, BANK:N_ALL], op=ALU.add
+            )
 
         NORM_AT = BATCH
         CHUNKS_AT = 2 * BATCH

@@ -253,7 +253,7 @@ def tile_ffnn_encoder_pa_t_kernel(
                 out=squares[:], in_=e[:], func=FUNC.Square, accum_out=sum_sq[:, b : b + 1]
             )
 
-        def normalise(e_tiles, sum_e, sum_sq):
+        def statistics(sum_e, sum_sq):
             total = work.tile([P, BATCH], F32, bufs=2)
             nc.gpsimd.tensor_tensor(out=total[:], in0=sum_e[:, :, 0], in1=sum_e[:, :, 1], op=ALU.add)
             minus_mean = work.tile([P, BATCH], F32, bufs=2)
@@ -271,15 +271,15 @@ def tile_ffnn_encoder_pa_t_kernel(
             nc.gpsimd.tensor_tensor(out=rstd[:], in0=var_eps[:], in1=minus_half[:], op=ALU.pow)
             shift = work.tile([P, BATCH], F32, bufs=2)
             nc.gpsimd.tensor_tensor(out=shift[:], in0=minus_mean[:], in1=rstd[:], op=ALU.mult)
-            normed_tiles = []
-            for b in range(BATCH):
-                normed = work.tile([P, D], F32, name="normed%d" % b, tag="normed", bufs=8)
-                nc.gpsimd.tensor_scalar(
-                    out=normed[:], in0=e_tiles[b][:], scalar1=rstd[:, b : b + 1],
-                    scalar2=shift[:, b : b + 1], op0=ALU.mult, op1=ALU.add,
-                )
-                normed_tiles.append(normed)
-            return normed_tiles
+            return rstd, shift
+
+        def normalise(e, b, rstd, shift):
+            normed = work.tile([P, D], F32, bufs=8)
+            nc.scalar.activation(
+                out=normed[:], in_=e[:], func=FUNC.Identity,
+                scale=rstd[:, b : b + 1], bias=shift[:, b : b + 1],
+            )
+            return normed
 
         def scale_and_shift(normed_tiles, c, planes):
             normed_t = psum_t.tile([P, GROUP], F32, tag="tp")
@@ -315,9 +315,8 @@ def tile_ffnn_encoder_pa_t_kernel(
 
         def project(b, h_mx, result):
             tokens = slice(b * P, (b + 1) * P)
-
-            def passes(acc, first):
-                width = acc.shape[1]
+            for name, first, width in (("acc_qk", 0, BANK), ("acc_v", BANK, N_ALL - BANK)):
+                acc = psum_o.tile([P, width], F32, name=name, tag=name)
                 for g in range(PASSES):
                     codes, scales = h_mx[g]
                     nc.tensor.matmul_mx(
@@ -329,23 +328,15 @@ def tile_ffnn_encoder_pa_t_kernel(
                         start=(g == 0),
                         stop=(g == PASSES - 1),
                     )
+                nc.vector.tensor_tensor(
+                    out=result[:, b, first : first + width], in0=acc[:],
+                    in1=bias_qkv[:, first : first + width], op=ALU.add,
+                )
 
-            acc_qk = psum_o.tile([P, BANK], F32)
-            passes(acc_qk, 0)
-            nc.vector.tensor_tensor(
-                out=result[:, b, 0:BANK], in0=acc_qk[:], in1=bias_qkv[:, 0:BANK], op=ALU.add
-            )
-            acc_v = psum_o.tile([P, N_ALL - BANK], F32)
-            passes(acc_v, BANK)
-            v_plain = work.tile([P, N_ALL - BANK], F32, bufs=4)
-            nc.scalar.copy(out=v_plain[:], in_=acc_v[:])
-            nc.gpsimd.tensor_tensor(
-                out=result[:, b, BANK:N_ALL], in0=v_plain[:], in1=bias_qkv[:, BANK:N_ALL], op=ALU.add
-            )
-
-        NORM_AT = BATCH
-        CHUNKS_AT = 2 * BATCH
-        PROJECT_AT = 3 * BATCH + 1
+        STATS_AT = BATCH
+        NORM_AT = STATS_AT + 1
+        CHUNKS_AT = NORM_AT + BATCH
+        PROJECT_AT = CHUNKS_AT + BATCH + 1
         CHUNKS_A_STEP = CHUNKS // BATCH
 
         def group_at(step, lag):
@@ -356,6 +347,7 @@ def tile_ffnn_encoder_pa_t_kernel(
         make_timing(0)
         sums_of = {}
         e_of = {}
+        stats_of = {}
         normed_of = {}
         h_mx_of = {}
         w_grouped_of = {}
@@ -375,9 +367,15 @@ def tile_ffnn_encoder_pa_t_kernel(
             if step + 1 < N_POS:
                 make_timing(step + 1)
 
-            done, place = group_at(step, NORM_AT)
+            done, place = group_at(step, STATS_AT)
             if done is not None and place == 0:
-                normed_of[done] = normalise(e_of[done], sums_of[done][0], sums_of[done][1])
+                stats_of[done] = statistics(sums_of[done][0], sums_of[done][1])
+                normed_of[done] = []
+            done, place = group_at(step, NORM_AT)
+            if done is not None:
+                normed_of[done].append(
+                    normalise(e_of[done][place], place, stats_of[done][0], stats_of[done][1])
+                )
             if group is not None and b == 1 and 1 <= group <= 3:
                 quantise_weight(group - 1, w_grouped_of[group - 1])
 

import math
from contextlib import ExitStack

import concourse.mybir as mybir
from concourse.masks import make_identity

F32 = mybir.dt.float32
BF16 = mybir.dt.bfloat16
I32 = mybir.dt.int32
U32 = mybir.dt.uint32
U8 = mybir.dt.uint8
FP8X4 = mybir.dt.float8_e4m3fn_x4
ALU = mybir.AluOpType
FUNC = mybir.ActivationFunctionType

P = 128
BATCH = 4
SEQ = 1024
FIN = 128
D = 1024
N_OUT = 256
N_ALL = 3 * N_OUT
EPS = 1e-3
BANK = 512
HALVES = D // BANK
PACK = 4
K_PASS = P * PACK
PASSES = D // K_PASS
CHUNKS = D // P
N_POS = SEQ // P
GROUP = BATCH * P

FLOPS = 2 * BATCH * SEQ * (FIN * D + D * N_ALL)

N_FREQ = D // 2
LOG_STEP = math.log(10000.0) / (N_FREQ - 1)
FINE = 32
COARSE = N_FREQ // FINE
HEAD_BITS = 12
ROUND_TO_INT = 12582912.0


def head_of(value):
    exponent = math.floor(math.log(value) / math.log(2.0))
    step = 2.0 ** (exponent - HEAD_BITS + 1)
    return round(value / step) * step


def fill_table(nc, heads, tails, one, values):
    for i, value in enumerate(values):
        nc.vector.memset(heads[:, i : i + 1], head_of(value))
        nc.scalar.mul(out=tails[:, i : i + 1], in_=one[:], mul=value - head_of(value))


def tile_ffnn_encoder_pa_t_kernel(
    tc, x, W_emb, b_emb, g0, beta0, Wq, bq, Wk, bk, Wv, bv, out_0, out_1, out_2
):
    nc = tc.nc
    with ExitStack() as ctx:
        ctx.enter_context(tc.manual_schedule())
        keep = ctx.enter_context(tc.tile_pool(name="keep", bufs=1))
        work = ctx.enter_context(tc.tile_pool(name="work", bufs=2))
        psum_z = ctx.enter_context(tc.psum_pool(name="psum_z", bufs=2))
        psum_t = ctx.enter_context(tc.psum_pool(name="psum_t", bufs=4))
        psum_o = ctx.enter_context(tc.psum_pool(name="psum_o", bufs=1))

        x_by_pos = x.rearrange("b (a p) f -> a p b f", p=P)
        x_sb = keep.tile([P, N_POS, BATCH, FIN], BF16)
        nc.sync.dma_start(out=x_sb[:, 0], in_=x_by_pos[0])
        w_emb = keep.tile([P, D], BF16)
        nc.sync.dma_start(out=w_emb[:], in_=W_emb)
        rows = keep.tile([P, P], BF16)
        nc.vector.memset(rows[:], 0.0)
        for v, vector in enumerate((b_emb, g0, beta0)):
            nc.sync.dma_start(
                out=rows[v * CHUNKS : (v + 1) * CHUNKS, :],
                in_=vector.rearrange("(c p) -> c p", p=P),
            )
        for a in range(1, N_POS):
            nc.sync.dma_start(out=x_sb[:, a], in_=x_by_pos[a])
        w_raw = []
        for w, weight in enumerate((Wq, Wk, Wv)):
            raw = keep.tile([P, PASSES, PACK, N_OUT], BF16, name="w_raw%d" % w)
            nc.sync.dma_start(
                out=raw[:].rearrange("p g t n -> p (g t) n"),
                in_=weight.rearrange("(c p) n -> p c n", p=P),
            )
            w_raw.append(raw)
        bias_qkv = keep.tile([P, N_ALL], BF16)
        for w, vector in enumerate((bq, bk, bv)):
            nc.sync.dma_start(
                out=bias_qkv[:, w * N_OUT : (w + 1) * N_OUT], in_=vector.partition_broadcast(P)
            )

        ident_b = keep.tile([P, P], BF16)
        make_identity(nc, ident_b[:])
        ident_f = keep.tile([P, P], F32)
        make_identity(nc, ident_f[:])
        pos_i = keep.tile([P, N_POS], I32)
        nc.gpsimd.iota(out=pos_i[:], pattern=[[P, N_POS]], base=0, channel_multiplier=1)
        one = keep.tile([P, 1], F32)
        nc.vector.memset(one[:], 1.0)
        minus_eighth = keep.tile([P, 1], F32)
        nc.vector.memset(minus_eighth[:], -0.125)
        plus_eighth = keep.tile([P, 1], F32)
        nc.vector.memset(plus_eighth[:], 0.125)
        minus_half = keep.tile([P, BATCH], F32)
        nc.vector.memset(minus_half[:], -0.5)
        quarter_turn = keep.tile([P, 1], F32)
        nc.scalar.mul(out=quarter_turn[:], in_=one[:], mul=0.5 * math.pi)

        coarse_hd = keep.tile([P, COARSE], F32)
        coarse_tl = keep.tile([P, COARSE], F32)
        fill_table(
            nc, coarse_hd, coarse_tl, one,
            [math.exp(-FINE * i * LOG_STEP) / (2.0 * math.pi) for i in range(COARSE)],
        )
        fine_hd = keep.tile([P, FINE], F32)
        fine_tl = keep.tile([P, FINE], F32)
        fill_table(nc, fine_hd, fine_tl, one, [math.exp(-i * LOG_STEP) for i in range(FINE)])

        def over_fine(table):
            return table[:].unsqueeze(2).to_broadcast([P, COARSE, FINE])

        def over_coarse(table):
            return table[:].unsqueeze(1).to_broadcast([P, COARSE, FINE])

        def as_grid(flat):
            return flat[:].rearrange("p (a b) -> p a b", b=FINE)

        product = keep.tile([P, N_FREQ], F32)
        cross = keep.tile([P, N_FREQ], F32)
        cross2 = keep.tile([P, N_FREQ], F32)
        f_head = keep.tile([P, N_FREQ], F32)
        f_tail = keep.tile([P, N_FREQ], F32)
        nc.vector.tensor_tensor(
            out=as_grid(product), in0=over_fine(coarse_hd), in1=over_coarse(fine_hd), op=ALU.mult
        )
        nc.vector.tensor_single_scalar(
            out=f_head[:].bitcast(I32), in_=product[:].bitcast(I32), scalar=-2048, op=ALU.bitwise_and
        )
        pos = keep.tile([P, N_POS], F32)
        nc.vector.tensor_copy(out=pos[:], in_=pos_i[:])
        fine_all = keep.tile([P, FINE], F32)
        nc.vector.tensor_tensor(out=fine_all[:], in0=fine_hd[:], in1=fine_tl[:], op=ALU.add)
        nc.vector.tensor_tensor(
            out=as_grid(cross), in0=over_fine(coarse_hd), in1=over_coarse(fine_tl), op=ALU.mult
        )
        nc.vector.tensor_tensor(
            out=as_grid(cross2), in0=over_fine(coarse_tl), in1=over_coarse(fine_all), op=ALU.mult
        )
        nc.vector.tensor_tensor(out=cross[:], in0=cross[:], in1=cross2[:], op=ALU.add)
        nc.vector.tensor_tensor(out=product[:], in0=product[:], in1=f_head[:], op=ALU.subtract)
        nc.vector.tensor_tensor(out=f_tail[:], in0=product[:], in1=cross[:], op=ALU.add)

        rows_t = psum_t.tile([P, P], BF16, tag="tp")
        nc.tensor.transpose(out=rows_t[:], in_=rows[:], identity=ident_b[:])
        cols = keep.tile([P, 3 * CHUNKS], F32)
        nc.vector.tensor_copy(out=cols[:], in_=rows_t[:, 0 : 3 * CHUNKS])
        b_wide = keep.tile([P, CHUNKS, P], F32)
        nc.vector.tensor_copy(
            out=b_wide[:], in_=cols[:, 0:CHUNKS].unsqueeze(2).to_broadcast([P, CHUNKS, P])
        )

        w_codes = keep.tile([P, PASSES, N_ALL], U32, align_bytes=64)
        w_scales = keep.tile([P, PASSES, N_ALL], U8, align_bytes=64)

        def regroup_weight(w):
            w_grouped = work.tile([P, PASSES, N_OUT, PACK], BF16, bufs=2, align_bytes=64)
            nc.scalar.copy(out=w_grouped[:], in_=w_raw[w][:].rearrange("p g t n -> p g n t"))
            return w_grouped

        def quantise_weight(w, w_grouped):
            for g in range(PASSES):
                cols_w = slice(w * N_OUT, (w + 1) * N_OUT)
                nc.vector.quantize_mx(
                    out=w_codes[:, g, cols_w].bitcast(FP8X4),
                    scales=w_scales[:, g, cols_w],
                    in_=w_grouped[:, g].rearrange("p n t -> p (n t)"),
                )

        timing = keep.tile([P, N_POS, D], F32)

        def make_timing(a):
            here = pos[:, a : a + 1]
            turns = work.tile([P, N_FREQ], F32, bufs=2)
            nc.vector.tensor_scalar(
                out=turns[:], in0=f_head[:], scalar1=here, scalar2=-0.125, op0=ALU.mult, op1=ALU.add
            )
            whole = work.tile([P, N_FREQ], F32, bufs=2)
            nc.vector.tensor_scalar(
                out=whole[:], in0=turns[:], scalar1=ROUND_TO_INT, scalar2=ROUND_TO_INT,
                op0=ALU.add, op1=ALU.subtract,
            )
            nc.vector.tensor_tensor(out=whole[:], in0=turns[:], in1=whole[:], op=ALU.subtract)
            frac = work.tile([P, N_FREQ], F32, bufs=2)
            nc.vector.scalar_tensor_tensor(
                out=frac[:], in0=f_tail[:], scalar=here, in1=whole[:], op0=ALU.mult, op1=ALU.add
            )
            distance = work.tile([P, D], F32, bufs=2)
            nc.scalar.activation(
                out=distance[:, 0:N_FREQ], in_=frac[:], func=FUNC.Abs, bias=minus_eighth[:], scale=1.0
            )
            nc.scalar.activation(
                out=distance[:, N_FREQ:D], in_=frac[:], func=FUNC.Abs, bias=plus_eighth[:], scale=1.0
            )
            nc.scalar.activation(
                out=timing[:, a, :], in_=distance[:], func=FUNC.Sin,
                bias=quarter_turn[:], scale=-2.0 * math.pi,
            )

        def transpose_x(a):
            x_t_ps = psum_t.tile([P, GROUP], BF16, tag="tp")
            for b in range(BATCH):
                nc.tensor.transpose(
                    out=x_t_ps[:, b * P : (b + 1) * P], in_=x_sb[:, a, b, :], identity=ident_b[:]
                )
            x_t = work.tile([P, GROUP], BF16, bufs=2)
            nc.scalar.copy(out=x_t[:], in_=x_t_ps[:])
            return x_t

        def embed_bank(a, b, half, x_t, e, sum_e):
            z = psum_z.tile([P, BANK], F32)
            for j in range(BANK // P):
                nc.tensor.matmul(
                    out=z[:, j * P : (j + 1) * P],
                    lhsT=b_wide[:, half * (BANK // P) + j, :],
                    rhs=ident_f[:],
                    is_transpose=True,
                    start=(j == 0),
                    stop=False,
                )
            nc.tensor.matmul(
                out=z[:],
                lhsT=x_t[:, b * P : (b + 1) * P],
                rhs=w_emb[:, half * BANK : (half + 1) * BANK],
                start=False,
                stop=True,
            )
            nc.vector.scalar_tensor_tensor(
                out=e[:, half * BANK : (half + 1) * BANK],
                in0=z[:],
                scalar=0.0,
                in1=timing[:, a, half * BANK : (half + 1) * BANK],
                op0=ALU.max,
                op1=ALU.add,
                accum_out=sum_e[:, b, half : half + 1],
            )

        def sum_of_squares(e, b, sum_sq):
            squares = work.tile([P, D], BF16, bufs=2)
            nc.scalar.activation(
                out=squares[:], in_=e[:], func=FUNC.Square, accum_out=sum_sq[:, b : b + 1]
            )

        def statistics(sum_e, sum_sq):
            total = work.tile([P, BATCH], F32, bufs=2)
            nc.gpsimd.tensor_tensor(out=total[:], in0=sum_e[:, :, 0], in1=sum_e[:, :, 1], op=ALU.add)
            minus_mean = work.tile([P, BATCH], F32, bufs=2)
            nc.gpsimd.tensor_scalar(
                out=minus_mean[:], in0=total[:], scalar1=-1.0 / D, scalar2=0.0, op0=ALU.mult, op1=ALU.add
            )
            mean_sq = work.tile([P, BATCH], F32, bufs=2)
            nc.gpsimd.tensor_tensor(out=mean_sq[:], in0=minus_mean[:], in1=minus_mean[:], op=ALU.mult)
            var_eps = work.tile([P, BATCH], F32, bufs=2)
            nc.gpsimd.tensor_scalar(
                out=var_eps[:], in0=sum_sq[:], scalar1=1.0 / D, scalar2=EPS, op0=ALU.mult, op1=ALU.add
            )
            nc.gpsimd.tensor_tensor(out=var_eps[:], in0=var_eps[:], in1=mean_sq[:], op=ALU.subtract)
            rstd = work.tile([P, BATCH], F32, bufs=2)
            nc.gpsimd.tensor_tensor(out=rstd[:], in0=var_eps[:], in1=minus_half[:], op=ALU.pow)
            shift = work.tile([P, BATCH], F32, bufs=2)
            nc.gpsimd.tensor_tensor(out=shift[:], in0=minus_mean[:], in1=rstd[:], op=ALU.mult)
            return rstd, shift

        def normalise(e, b, rstd, shift):
            normed = work.tile([P, D], F32, bufs=8)
            nc.scalar.activation(
                out=normed[:], in_=e[:], func=FUNC.Identity,
                scale=rstd[:, b : b + 1], bias=shift[:, b : b + 1],
            )
            return normed

        def scale_and_shift(normed_tiles, c, planes):
            normed_t = psum_t.tile([P, GROUP], F32, tag="tp")
            for b in range(BATCH):
                nc.tensor.transpose(
                    out=normed_t[:, b * P : (b + 1) * P],
                    in_=normed_tiles[b][:, c * P : (c + 1) * P],
                    identity=ident_f[:],
                )
            nc.scalar.activation(
                out=planes[:, c % PACK, :], in_=normed_t[:], func=FUNC.Identity,
                scale=cols[:, CHUNKS + c : CHUNKS + c + 1],
                bias=cols[:, 2 * CHUNKS + c : 2 * CHUNKS + c + 1],
            )

        def regroup(planes):
            grouped = work.tile([P, GROUP, PACK], BF16, bufs=2, align_bytes=64)
            nc.vector.tensor_copy(
                out=grouped[:].rearrange("p (c i) t -> p c t i", i=PACK),
                in_=planes[:].rearrange("p t (c i) -> p c t i", i=PACK),
            )
            return grouped

        def quantise(grouped):
            codes = work.tile([P, GROUP], U32, bufs=4, align_bytes=64)
            scales = work.tile([P, GROUP], U8, bufs=4, align_bytes=64)
            nc.vector.quantize_mx(
                out=codes[:].bitcast(FP8X4),
                scales=scales[:],
                in_=grouped[:].rearrange("p r t -> p (r t)"),
            )
            return codes, scales

        def project(b, h_mx, result):
            tokens = slice(b * P, (b + 1) * P)
            for name, first, width in (("acc_qk", 0, BANK), ("acc_v", BANK, N_ALL - BANK)):
                acc = psum_o.tile([P, width], F32, name=name, tag=name)
                for g in range(PASSES):
                    codes, scales = h_mx[g]
                    nc.tensor.matmul_mx(
                        out=acc[:],
                        lhsT=codes[:, tokens].bitcast(FP8X4),
                        lhsT_scale=scales[:, tokens],
                        rhs=w_codes[:, g, first : first + width].bitcast(FP8X4),
                        rhs_scale=w_scales[:, g, first : first + width],
                        start=(g == 0),
                        stop=(g == PASSES - 1),
                    )
                nc.vector.tensor_tensor(
                    out=result[:, b, first : first + width], in0=acc[:],
                    in1=bias_qkv[:, first : first + width], op=ALU.add,
                )

        STATS_AT = BATCH
        NORM_AT = STATS_AT + 1
        CHUNKS_AT = NORM_AT + BATCH
        PROJECT_AT = CHUNKS_AT + BATCH + 1
        CHUNKS_A_STEP = CHUNKS // BATCH

        def group_at(step, lag):
            group, place = divmod(step - lag, BATCH)
            return (group if 0 <= group < N_POS else None), place

        x_t_of = {0: transpose_x(0)}
        make_timing(0)
        sums_of = {}
        e_of = {}
        stats_of = {}
        normed_of = {}
        h_mx_of = {}
        w_grouped_of = {}
        waiting = None
        for step in range(BATCH * N_POS + PROJECT_AT):
            group, b = group_at(step, 0)
            if group is not None:
                if b == 0:
                    sum_e = work.tile([P, BATCH, HALVES], F32, bufs=3)
                    sum_sq = work.tile([P, BATCH], F32, bufs=3)
                    sums_of[group] = (sum_e, sum_sq)
                    e_of[group] = []
                e = work.tile([P, D], F32, bufs=8)
                e_of[group].append(e)
                for half in range(HALVES):
                    embed_bank(group, b, half, x_t_of[group], e, sums_of[group][0])
            if step + 1 < N_POS:
                make_timing(step + 1)

            done, place = group_at(step, STATS_AT)
            if done is not None and place == 0:
                stats_of[done] = statistics(sums_of[done][0], sums_of[done][1])
                normed_of[done] = []
            done, place = group_at(step, NORM_AT)
            if done is not None:
                normed_of[done].append(
                    normalise(e_of[done][place], place, stats_of[done][0], stats_of[done][1])
                )
            if group is not None and b == 1 and 1 <= group <= 3:
                quantise_weight(group - 1, w_grouped_of[group - 1])

            grouped = None
            if waiting is not None:
                grouped = regroup(waiting[1])
            turned, j = group_at(step, CHUNKS_AT)
            if turned is not None:
                for c in range(j * CHUNKS_A_STEP, (j + 1) * CHUNKS_A_STEP):
                    if c == 0:
                        h_mx_of[turned] = []
                    if c % PACK == 0:
                        planes = work.tile([P, PACK, GROUP], BF16, bufs=2)
                    scale_and_shift(normed_of[turned], c, planes)

            if group is not None:
                sum_of_squares(e, b, sums_of[group][1])
                if b == 2 and group + 1 < N_POS:
                    x_t_of[group + 1] = transpose_x(group + 1)
                if b == 3 and group < 3:
                    w_grouped_of[group] = regroup_weight(group)

            ready, tile_b = group_at(step, PROJECT_AT)
            if ready is not None:
                if tile_b == 0:
                    result = work.tile([P, BATCH, N_ALL], F32, bufs=2)
                project(tile_b, h_mx_of[ready], result)
                if tile_b == BATCH - 1:
                    for w, out in enumerate((out_0, out_1, out_2)):
                        nc.sync.dma_start(
                            out=out.rearrange("b (a p) n -> a p b n", p=P)[ready],
                            in_=result[:, :, w * N_OUT : (w + 1) * N_OUT],
                        )
            if grouped is not None:
                h_mx_of[waiting[0]].append(quantise(grouped))
                waiting = None
            if turned is not None and (j + 1) * CHUNKS_A_STEP % PACK == 0:
                waiting = (turned, planes)
